import numpy as np
import ml_dtypes


def mxq(x, axis, fmt="e4m3"):
    dtype, down = {"e4m3": (ml_dtypes.float8_e4m3fn, 7), "e5m2": (ml_dtypes.float8_e5m2, 14)}[fmt]
    v = np.moveaxis(np.asarray(x, np.float32).astype(ml_dtypes.bfloat16).astype(np.float64), axis, -1)
    blocks = v.reshape(v.shape[:-1] + (-1, 32))
    amax = np.abs(blocks).max(-1, keepdims=True)
    byte = np.maximum(np.where(amax > 0, np.frexp(amax)[1] - 1 + 127, 0) - down, 1)
    scale = np.exp2(byte - 127.0)
    codes = (blocks / scale).astype(np.float32).astype(dtype).astype(np.float64)
    return np.moveaxis((codes * scale).reshape(v.shape), -1, axis)


WIDE = False


def mx_kscale(k):
    if not WIDE:
        return np.ones(k)
    levels = np.array([10, -10, 5, -5, 0])
    a = np.random.permutation(np.resize(levels, k // 512 * 4)).reshape(k // 512, 4)
    idx = np.arange(k)
    return np.exp2(a[idx // 512, idx % 128 // 32])


BF16 = ml_dtypes.bfloat16


def bf(x):
    return np.asarray(x, np.float32).astype(BF16)


def f64(x):
    return np.asarray(x).astype(np.float64)


B, IN, H = 128, 7680, 512
D = IN + H
LN_EPS = 1e-5
DIV_EPS = 1e-6


def sigmoid(v):
    return 1.0 / (1.0 + np.exp(-v))


def setup_inputs():
    s = mx_kscale(D)
    d = {"x": bf(np.random.standard_normal((B, IN)) * s[:IN]),
         "h_prev": bf(np.random.standard_normal((B, H)) * s[IN:]),
         "c_prev": bf(np.random.standard_normal((B, H))),
         "n_prev": bf(np.random.uniform(0.0, 1.0, (B, H))),
         "m_prev": bf(np.random.uniform(0.0, 1.0, (B, H)))}
    for g in "ifoz":
        d["W" + g] = bf(np.random.standard_normal((H, D)) * 0.6 / np.sqrt(D) / s)
        d["b" + g] = bf(np.random.standard_normal(H) * 0.3)
    d["ln_gamma"] = bf(1.0 + 0.1 * np.random.standard_normal(H))
    d["ln_beta"] = bf(0.1 * np.random.standard_normal(H))
    return d


def reference(x, h_prev, c_prev, n_prev, m_prev, Wi, bi, Wf, bf, Wo, bo, Wz, bz, ln_gamma, ln_beta):
    combined = np.concatenate([f64(x), f64(h_prev)], axis=1)
    W = np.stack([f64(Wi), f64(Wf), f64(Wo), f64(Wz)], axis=0)
    b = np.stack([f64(bi), f64(bf), f64(bo), f64(bz)], axis=0)
    gates = (mxq(combined, 1, "e4m3") @ mxq(W, 2, "e4m3").transpose(0, 2, 1)) + b[:, None, :]
    i_t = np.exp(gates[0])
    f_t = sigmoid(gates[1])
    o_t = sigmoid(gates[2])
    z_t = np.tanh(gates[3])
    c_t = f_t * f64(c_prev) + i_t * z_t
    n_t = f_t * f64(n_prev) + i_t
    m_t = np.maximum(f_t * f64(m_prev), np.abs(i_t * z_t))
    h = o_t * (c_t / (n_t + DIV_EPS))
    mu = np.mean(h, axis=-1, keepdims=True)
    var = np.mean(np.square(h - mu), axis=-1, keepdims=True)
    h_t = (h - mu) * (1.0 / np.sqrt(var + LN_EPS)) * f64(ln_gamma) + f64(ln_beta)
    return (h_t, c_t, n_t, m_t)

@@ -1,0 +1,292 @@
+from contextlib import ExitStack
+
+import concourse.mybir as mybir
+from concourse.masks import make_identity
+
+F32 = mybir.dt.float32
+BF16 = mybir.dt.bfloat16
+I32 = mybir.dt.int32
+U32 = mybir.dt.uint32
+U8 = mybir.dt.uint8
+FP8X4 = mybir.dt.float8_e4m3fn_x4
+ALU = mybir.AluOpType
+ACT = mybir.ActivationFunctionType
+
+P = 128
+IN = 7680
+H = 512
+D = IN + H
+LN_EPS = 1e-5
+DIV_EPS = 1e-6
+
+PACK = 4
+K_PASS = P * PACK
+PASSES = D // K_PASS
+K_SLAB = 4096
+PASSES_PER_SLAB = K_SLAB // K_PASS
+SLABS_PER_BLOCK = D // K_SLAB
+BANK_WORDS = 512
+PASSES_PER_BANK = BANK_WORDS // (2 * P)
+BANKS_PER_SLAB = PASSES_PER_SLAB // PASSES_PER_BANK
+
+GATES = ("f", "i", "z", "o")
+BLOCKS_PER_GATE = H // P
+W_SLABS = len(GATES) * BLOCKS_PER_GATE * SLABS_PER_BLOCK
+
+TRANSPOSE_BANKS = 6
+VECTOR_TURN = 6
+PREFETCH = 8
+
+FLOPS = 2 * P * D * len(GATES) * H
+
+
+def tile_slstmcell_k_kernel(
+    tc, x, h_prev, c_prev, n_prev, m_prev, Wi, bi, Wf, bf, Wo, bo, Wz, bz, ln_gamma, ln_beta,
+    out_0, out_1, out_2, out_3,
+):
+    nc = tc.nc
+    weights = {"f": Wf, "i": Wi, "z": Wz, "o": Wo}
+    row_vectors = {"f": bf, "i": bi, "z": bz, "o": bo, "gamma": ln_gamma, "beta": ln_beta}
+    previous = {"c": c_prev, "n": n_prev, "m": m_prev}
+
+    with ExitStack() as ctx:
+        ctx.enter_context(tc.manual_schedule())
+        keep = ctx.enter_context(tc.tile_pool(name="keep", bufs=1))
+        raw_pool = ctx.enter_context(tc.tile_pool(name="raw", bufs=PREFETCH + 2))
+        grouped_pool = ctx.enter_context(tc.tile_pool(name="grouped", bufs=3))
+        quantised_pool = ctx.enter_context(tc.tile_pool(name="quantised", bufs=3))
+        small_pool = ctx.enter_context(tc.tile_pool(name="small", bufs=3))
+        bank_pool = ctx.enter_context(tc.psum_pool(name="banks", bufs=TRANSPOSE_BANKS))
+        sum_pool = ctx.enter_context(tc.psum_pool(name="sums", bufs=2))
+
+        identity = keep.tile([P, P], F32, name="identity")
+        make_identity(nc, identity[:])
+        ones = keep.tile([P, P], BF16, name="ones")
+        nc.vector.memset(ones[:], 1.0)
+        minus_half = keep.tile([P, 1], F32, name="minus_half")
+        nc.vector.memset(minus_half[:], -0.5)
+        vector_rows = keep.tile([P, len(row_vectors) * H], BF16, name="vector_rows")
+        nc.vector.memset(vector_rows[:].bitcast(I32), 0)
+
+        for v, name in enumerate(row_vectors):
+            nc.scalar.dma_start(
+                out=vector_rows[0:1, v * H : (v + 1) * H], in_=row_vectors[name].unsqueeze(0)
+            )
+        previous_bf16 = {}
+        for name in previous:
+            previous_bf16[name] = keep.tile([P, H], BF16, name="previous_" + name)
+            nc.scalar.dma_start(out=previous_bf16[name][:], in_=previous[name])
+        table_warmer = keep.tile([P, 1], F32, name="table_warmer")
+        nc.scalar.activation(out=table_warmer[:], in_=minus_half[:], func=ACT.Tanh)
+
+        def load_combined_slab(s):
+            raw = raw_pool.tile([P, K_SLAB], BF16, name="raw")
+            first_k = s * K_SLAB
+            from_x = min(IN - first_k, K_SLAB)
+            nc.sync.dma_start(out=raw[:, 0:from_x], in_=x[:, first_k : first_k + from_x])
+            if from_x < K_SLAB:
+                nc.sync.dma_start(out=raw[:, from_x:K_SLAB], in_=h_prev)
+            return raw
+
+        def load_weight_slab(t):
+            block, s = divmod(t, SLABS_PER_BLOCK)
+            gate, j = divmod(block, BLOCKS_PER_GATE)
+            raw = raw_pool.tile([P, K_SLAB], BF16, name="raw")
+            nc.sync.dma_start(
+                out=raw[:],
+                in_=weights[GATES[gate]][j * P : (j + 1) * P, s * K_SLAB : (s + 1) * K_SLAB],
+            )
+            return raw
+
+        def empty_bank(turn, out, in_):
+            if turn % VECTOR_TURN == 0:
+                nc.vector.tensor_copy(out=out, in_=in_)
+            else:
+                nc.scalar.copy(out=out, in_=in_)
+
+        def transpose_slab(raw, first_turn):
+            raw_words = raw[:].bitcast(F32)
+            grouped = grouped_pool.tile([P, K_SLAB], BF16, name="grouped", align_bytes=64)
+            grouped_words = grouped[:].bitcast(F32)
+            for b in range(BANKS_PER_SLAB):
+                bank = bank_pool.tile([P, 2, BANK_WORDS // 2], F32, name="bank")
+                for g in range(PASSES_PER_BANK):
+                    for u in range(2):
+                        first_word = ((b * PASSES_PER_BANK + g) * 2 + u) * P
+                        nc.tensor.transpose(
+                            bank[:, u, g * P : (g + 1) * P],
+                            raw_words[:, first_word : first_word + P],
+                            identity[:],
+                        )
+                empty_bank(
+                    first_turn + b,
+                    out=grouped_words[:, b * BANK_WORDS : (b + 1) * BANK_WORDS].rearrange(
+                        "p (c u) -> p c u", u=2
+                    ),
+                    in_=bank[:].rearrange("p u c -> p c u"),
+                )
+            return grouped
+
+        def quantise_slab(grouped, codes, scales):
+            nc.vector.quantize_mx(out=codes.bitcast(FP8X4), scales=scales, in_=grouped[:])
+
+        raw_combined = [load_combined_slab(s) for s in range(SLABS_PER_BLOCK)]
+        raw_weights = {}
+        for t in range(PREFETCH):
+            raw_weights[t] = load_weight_slab(t)
+
+        slab_words = PASSES_PER_SLAB * P
+        x_codes = keep.tile([P, PASSES * P], U32, name="x_codes", align_bytes=64)
+        x_scales = keep.tile([P, PASSES * P], U8, name="x_scales", align_bytes=64)
+        grouped_combined = [
+            transpose_slab(raw_combined[s], s * BANKS_PER_SLAB) for s in range(SLABS_PER_BLOCK)
+        ]
+        for s in range(SLABS_PER_BLOCK):
+            words = slice(s * slab_words, (s + 1) * slab_words)
+            quantise_slab(grouped_combined[s], x_codes[:, words], x_scales[:, words])
+
+        spread = {}
+        for v, name in enumerate(row_vectors):
+            bank = bank_pool.tile([P, H], F32, name="bank")
+            nc.tensor.matmul(
+                out=bank[:], lhsT=ones[:], rhs=vector_rows[:, v * H : (v + 1) * H],
+                start=True, stop=True,
+            )
+            spread[name] = keep.tile([P, H], F32, name="spread_" + name)
+            empty_bank(v + 1, out=spread[name][:], in_=bank[:])
+
+        half_previous = {}
+        for name in previous:
+            half_previous[name] = keep.tile([P, H], F32, name="half_previous_" + name)
+            nc.gpsimd.tensor_scalar(
+                out=half_previous[name][:], in0=previous_bf16[name][:],
+                scalar1=0.5, scalar2=0.0, op0=ALU.mult, op1=ALU.add,
+            )
+
+        full = {}
+        for name in (
+            "tanh_f", "f_c", "f_n", "f_m", "i", "denominator", "reciprocal", "n_t", "z", "i_z",
+            "abs_i_z", "c_t", "m_t", "half_ratio", "tanh_o", "h", "centred", "h_t",
+        ):
+            full[name] = keep.tile([P, H], F32, name=name)
+        stats = keep.tile([P, BLOCKS_PER_GATE, 6], F32, name="stats")
+
+        def activate(gate, cols, sums):
+            biased = small_pool.tile([P, P], F32, name="biased")
+            nc.vector.tensor_add(out=biased[:], in0=sums[:], in1=spread[gate][:, cols])
+            if gate == "f":
+                nc.scalar.activation(out=full["tanh_f"][:, cols], in_=biased[:], func=ACT.Tanh, scale=0.5)
+            if gate == "i":
+                nc.scalar.activation(out=full["i"][:, cols], in_=biased[:], func=ACT.Exp)
+            if gate == "z":
+                nc.scalar.activation(out=full["z"][:, cols], in_=biased[:], func=ACT.Tanh)
+            if gate == "o":
+                nc.scalar.activation(out=full["tanh_o"][:, cols], in_=biased[:], func=ACT.Tanh, scale=0.5)
+
+        def combine(gate, j, cols):
+            if gate == "f":
+                for name in previous:
+                    nc.vector.scalar_tensor_tensor(
+                        out=full["f_" + name][:, cols], in0=full["tanh_f"][:, cols], scalar=1.0,
+                        in1=half_previous[name][:, cols], op0=ALU.add, op1=ALU.mult,
+                    )
+            if gate == "i":
+                nc.vector.scalar_tensor_tensor(
+                    out=full["denominator"][:, cols], in0=full["i"][:, cols], scalar=DIV_EPS,
+                    in1=full["f_n"][:, cols], op0=ALU.add, op1=ALU.add,
+                )
+                nc.vector.tensor_add(
+                    out=full["n_t"][:, cols], in0=full["f_n"][:, cols], in1=full["i"][:, cols]
+                )
+                nc.vector.reciprocal(out=full["reciprocal"][:, cols], in_=full["denominator"][:, cols])
+            if gate == "z":
+                nc.vector.tensor_mul(
+                    out=full["i_z"][:, cols], in0=full["i"][:, cols], in1=full["z"][:, cols]
+                )
+                nc.scalar.activation(out=full["abs_i_z"][:, cols], in_=full["i_z"][:, cols], func=ACT.Abs)
+                nc.vector.tensor_add(
+                    out=full["c_t"][:, cols], in0=full["f_c"][:, cols], in1=full["i_z"][:, cols]
+                )
+                nc.vector.scalar_tensor_tensor(
+                    out=full["half_ratio"][:, cols], in0=full["c_t"][:, cols], scalar=0.5,
+                    in1=full["reciprocal"][:, cols], op0=ALU.mult, op1=ALU.mult,
+                )
+                nc.vector.tensor_max(
+                    out=full["m_t"][:, cols], in0=full["f_m"][:, cols], in1=full["abs_i_z"][:, cols]
+                )
+            if gate == "o":
+                nc.vector.scalar_tensor_tensor(
+                    out=full["h"][:, cols], in0=full["tanh_o"][:, cols], scalar=1.0,
+                    in1=full["half_ratio"][:, cols], op0=ALU.add, op1=ALU.mult,
+                )
+                nc.vector.bn_stats(out=stats[:, j, :], in_=full["h"][:, cols])
+            if j == BLOCKS_PER_GATE - 1:
+                if gate == "i":
+                    nc.sync.dma_start(out=out_2, in_=full["n_t"][:])
+                if gate == "z":
+                    nc.sync.dma_start(out=out_1, in_=full["c_t"][:])
+                    nc.sync.dma_start(out=out_3, in_=full["m_t"][:])
+
+        def block_of(t):
+            gate, j = divmod(t // SLABS_PER_BLOCK, BLOCKS_PER_GATE)
+            return GATES[gate], j, slice(j * P, (j + 1) * P)
+
+        grouped_weights = {}
+        w_codes = {}
+        w_scales = {}
+        sums = {}
+        for step in range(W_SLABS + 3):
+            if step + PREFETCH < W_SLABS:
+                raw_weights[step + PREFETCH] = load_weight_slab(step + PREFETCH)
+            if step < W_SLABS:
+                grouped_weights[step] = transpose_slab(raw_weights[step], step * BANKS_PER_SLAB)
+
+            t = step - 1
+            if 0 <= t < W_SLABS:
+                w_codes[t] = quantised_pool.tile([P, slab_words], U32, name="w_codes", align_bytes=64)
+                w_scales[t] = quantised_pool.tile([P, slab_words], U8, name="w_scales", align_bytes=64)
+                quantise_slab(grouped_weights[t], w_codes[t][:], w_scales[t][:])
+
+            t = step - 2
+            if 0 <= t < W_SLABS:
+                block, s = divmod(t, SLABS_PER_BLOCK)
+                if s == 0:
+                    sums[block] = sum_pool.tile([P, P], F32, name="sums")
+                for q in range(PASSES_PER_SLAB):
+                    k_pass = s * PASSES_PER_SLAB + q
+                    x_words = slice(k_pass * P, (k_pass + 1) * P)
+                    w_words = slice(q * P, (q + 1) * P)
+                    nc.tensor.matmul_mx(
+                        out=sums[block][:],
+                        lhsT=x_codes[:, x_words].bitcast(FP8X4),
+                        lhsT_scale=x_scales[:, x_words],
+                        rhs=w_codes[t][:, w_words].bitcast(FP8X4),
+                        rhs_scale=w_scales[t][:, w_words],
+                        start=(k_pass == 0),
+                        stop=(k_pass == PASSES - 1),
+                    )
+
+            t = step - 3
+            if 0 <= t < W_SLABS and t % SLABS_PER_BLOCK == SLABS_PER_BLOCK - 1:
+                gate, j, cols = block_of(t)
+                combine(gate, j, cols)
+            t = step - 2
+            if 0 <= t < W_SLABS and t % SLABS_PER_BLOCK == SLABS_PER_BLOCK - 1:
+                gate, j, cols = block_of(t)
+                activate(gate, cols, sums[t // SLABS_PER_BLOCK])
+
+        mean_var = keep.tile([P, 2], F32, name="mean_var")
+        nc.vector.bn_aggr(out=mean_var[:], in_=stats[:].rearrange("p j s -> p (j s)"))
+        var_eps = keep.tile([P, 1], F32, name="var_eps")
+        nc.vector.tensor_scalar_add(out=var_eps[:], in0=mean_var[:, 1:2], scalar1=LN_EPS)
+        inv_std = keep.tile([P, 1], F32, name="inv_std")
+        nc.gpsimd.tensor_tensor(out=inv_std[:], in0=var_eps[:], in1=minus_half[:], op=ALU.pow)
+        nc.vector.scalar_tensor_tensor(
+            out=full["centred"][:], in0=full["h"][:], scalar=mean_var[:, 0:1],
+            in1=spread["gamma"][:], op0=ALU.subtract, op1=ALU.mult,
+        )
+        nc.vector.scalar_tensor_tensor(
+            out=full["h_t"][:], in0=full["centred"][:], scalar=inv_std[:],
+            in1=spread["beta"][:], op0=ALU.mult, op1=ALU.add,
+        )
+        nc.sync.dma_start(out=out_0, in_=full["h_t"][:])

@@ -22,22 +22,28 @@ DIV_EPS = 1e-6
 PACK = 4
 K_PASS = P * PACK
 PASSES = D // K_PASS
-K_SLAB = 4096
-PASSES_PER_SLAB = K_SLAB // K_PASS
-SLABS_PER_BLOCK = D // K_SLAB
 BANK_WORDS = 512
 PASSES_PER_BANK = BANK_WORDS // (2 * P)
-BANKS_PER_SLAB = PASSES_PER_SLAB // PASSES_PER_BANK
 
 GATES = ("f", "i", "z", "o")
 BLOCKS_PER_GATE = H // P
-W_SLABS = len(GATES) * BLOCKS_PER_GATE * SLABS_PER_BLOCK
+BLOCKS = len(GATES) * BLOCKS_PER_GATE
 
 TRANSPOSE_BANKS = 6
-VECTOR_TURN = 6
 PREFETCH = 8
+MULTIPLY_LAG = 2
 
 FLOPS = 2 * P * D * len(GATES) * H
+
+
+def piece_sizes(taper):
+    sizes = [PASSES // 2]
+    rest = PASSES // 2
+    while taper and rest > PASSES_PER_BANK:
+        rest = rest // 2
+        sizes.append(rest)
+    sizes.append(rest)
+    return sizes
 
 
 def tile_slstmcell_k_kernel(
@@ -53,8 +59,8 @@ def tile_slstmcell_k_kernel(
         ctx.enter_context(tc.manual_schedule())
         keep = ctx.enter_context(tc.tile_pool(name="keep", bufs=1))
         raw_pool = ctx.enter_context(tc.tile_pool(name="raw", bufs=PREFETCH + 2))
-        grouped_pool = ctx.enter_context(tc.tile_pool(name="grouped", bufs=3))
-        quantised_pool = ctx.enter_context(tc.tile_pool(name="quantised", bufs=3))
+        grouped_pool = ctx.enter_context(tc.tile_pool(name="grouped", bufs=5))
+        quantised_pool = ctx.enter_context(tc.tile_pool(name="quantised", bufs=5))
         small_pool = ctx.enter_context(tc.tile_pool(name="small", bufs=3))
         bank_pool = ctx.enter_context(tc.psum_pool(name="banks", bufs=TRANSPOSE_BANKS))
         sum_pool = ctx.enter_context(tc.psum_pool(name="sums", bufs=2))
@@ -67,93 +73,105 @@ def tile_slstmcell_k_kernel(
         nc.vector.memset(minus_half[:], -0.5)
         vector_rows = keep.tile([P, len(row_vectors) * H], BF16, name="vector_rows")
         nc.vector.memset(vector_rows[:].bitcast(I32), 0)
+        table_warmer = keep.tile([P, 1], F32, name="table_warmer")
+        nc.scalar.activation(out=table_warmer[:], in_=minus_half[:], func=ACT.Tanh)
 
         for v, name in enumerate(row_vectors):
-            nc.scalar.dma_start(
+            nc.gpsimd.dma_start(
                 out=vector_rows[0:1, v * H : (v + 1) * H], in_=row_vectors[name].unsqueeze(0)
             )
         previous_bf16 = {}
         for name in previous:
             previous_bf16[name] = keep.tile([P, H], BF16, name="previous_" + name)
-            nc.scalar.dma_start(out=previous_bf16[name][:], in_=previous[name])
-        table_warmer = keep.tile([P, 1], F32, name="table_warmer")
-        nc.scalar.activation(out=table_warmer[:], in_=minus_half[:], func=ACT.Tanh)
+            nc.gpsimd.dma_start(out=previous_bf16[name][:], in_=previous[name])
 
-        def load_combined_slab(s):
-            raw = raw_pool.tile([P, K_SLAB], BF16, name="raw")
-            first_k = s * K_SLAB
-            from_x = min(IN - first_k, K_SLAB)
-            nc.sync.dma_start(out=raw[:, 0:from_x], in_=x[:, first_k : first_k + from_x])
-            if from_x < K_SLAB:
-                nc.sync.dma_start(out=raw[:, from_x:K_SLAB], in_=h_prev)
-            return raw
+        pieces = []
+        for block in range(BLOCKS):
+            first_pass = 0
+            for n_passes in piece_sizes(block == BLOCKS - 1):
+                pieces.append((block, first_pass, n_passes))
+                first_pass += n_passes
 
-        def load_weight_slab(t):
-            block, s = divmod(t, SLABS_PER_BLOCK)
+        raw_at = {}
+
+        def load_rows(block, first_pass, n_passes, sources):
+            raw = raw_pool.tile([P, n_passes * K_PASS], BF16, name="raw")
+            column = 0
+            for source in sources:
+                nc.sync.dma_start(out=raw[:, column : column + source.shape[1]], in_=source)
+                column += source.shape[1]
+            for q in range(n_passes):
+                raw_at[(block, first_pass + q)] = (raw, q * K_PASS)
+
+        def load_weight_piece(t):
+            block, first_pass, n_passes = pieces[t]
             gate, j = divmod(block, BLOCKS_PER_GATE)
-            raw = raw_pool.tile([P, K_SLAB], BF16, name="raw")
-            nc.sync.dma_start(
-                out=raw[:],
-                in_=weights[GATES[gate]][j * P : (j + 1) * P, s * K_SLAB : (s + 1) * K_SLAB],
-            )
-            return raw
+            k_range = slice(first_pass * K_PASS, (first_pass + n_passes) * K_PASS)
+            load_rows(block, first_pass, n_passes, [weights[GATES[gate]][j * P : (j + 1) * P, k_range]])
 
-        def empty_bank(turn, out, in_):
-            if turn % VECTOR_TURN == 0:
-                nc.vector.tensor_copy(out=out, in_=in_)
-            else:
-                nc.scalar.copy(out=out, in_=in_)
+        COMBINED = -1
+        half_k = D // 2
+        load_rows(COMBINED, 0, PASSES // 2, [x[:, 0:half_k]])
+        load_rows(COMBINED, PASSES // 2, PASSES // 2, [x[:, half_k:IN], h_prev])
+        for t in range(PREFETCH):
+            load_weight_piece(t)
 
-        def transpose_slab(raw, first_turn):
-            raw_words = raw[:].bitcast(F32)
-            grouped = grouped_pool.tile([P, K_SLAB], BF16, name="grouped", align_bytes=64)
+        def transpose_piece(block, first_pass, n_passes):
+            grouped = grouped_pool.tile([P, n_passes * K_PASS], BF16, name="grouped", align_bytes=64)
             grouped_words = grouped[:].bitcast(F32)
-            for b in range(BANKS_PER_SLAB):
+            n_banks = n_passes // PASSES_PER_BANK
+            left_for_vector = None
+            for b in range(n_banks):
                 bank = bank_pool.tile([P, 2, BANK_WORDS // 2], F32, name="bank")
                 for g in range(PASSES_PER_BANK):
+                    raw, column = raw_at[(block, first_pass + b * PASSES_PER_BANK + g)]
+                    pass_words = raw[:, column : column + K_PASS].bitcast(F32)
                     for u in range(2):
-                        first_word = ((b * PASSES_PER_BANK + g) * 2 + u) * P
                         nc.tensor.transpose(
                             bank[:, u, g * P : (g + 1) * P],
-                            raw_words[:, first_word : first_word + P],
+                            pass_words[:, u * P : (u + 1) * P],
                             identity[:],
                         )
-                empty_bank(
-                    first_turn + b,
-                    out=grouped_words[:, b * BANK_WORDS : (b + 1) * BANK_WORDS].rearrange(
-                        "p (c u) -> p c u", u=2
-                    ),
-                    in_=bank[:].rearrange("p u c -> p c u"),
+                out = grouped_words[:, b * BANK_WORDS : (b + 1) * BANK_WORDS].rearrange(
+                    "p (c u) -> p c u", u=2
                 )
-            return grouped
+                in_ = bank[:].rearrange("p u c -> p c u")
+                if b == n_banks - 1 and first_pass == 0:
+                    left_for_vector = (out, in_)
+                else:
+                    nc.scalar.copy(out=out, in_=in_)
+            return grouped, left_for_vector
 
-        def quantise_slab(grouped, codes, scales):
+        def vector_empties(left_for_vector):
+            if left_for_vector is not None:
+                nc.vector.tensor_copy(out=left_for_vector[0], in_=left_for_vector[1])
+
+        def quantise_piece(grouped, codes, scales):
             nc.vector.quantize_mx(out=codes.bitcast(FP8X4), scales=scales, in_=grouped[:])
 
-        raw_combined = [load_combined_slab(s) for s in range(SLABS_PER_BLOCK)]
-        raw_weights = {}
-        for t in range(PREFETCH):
-            raw_weights[t] = load_weight_slab(t)
-
-        slab_words = PASSES_PER_SLAB * P
         x_codes = keep.tile([P, PASSES * P], U32, name="x_codes", align_bytes=64)
         x_scales = keep.tile([P, PASSES * P], U8, name="x_scales", align_bytes=64)
-        grouped_combined = [
-            transpose_slab(raw_combined[s], s * BANKS_PER_SLAB) for s in range(SLABS_PER_BLOCK)
-        ]
-        for s in range(SLABS_PER_BLOCK):
-            words = slice(s * slab_words, (s + 1) * slab_words)
-            quantise_slab(grouped_combined[s], x_codes[:, words], x_scales[:, words])
+        for first_pass in (0, PASSES // 2):
+            grouped, left_for_vector = transpose_piece(COMBINED, first_pass, PASSES // 2)
+            vector_empties(left_for_vector)
+            words = slice(first_pass * P, (first_pass + PASSES // 2) * P)
+            quantise_piece(grouped, x_codes[:, words], x_scales[:, words])
 
         spread = {}
-        for v, name in enumerate(row_vectors):
-            bank = bank_pool.tile([P, H], F32, name="bank")
-            nc.tensor.matmul(
-                out=bank[:], lhsT=ones[:], rhs=vector_rows[:, v * H : (v + 1) * H],
-                start=True, stop=True,
-            )
-            spread[name] = keep.tile([P, H], F32, name="spread_" + name)
-            empty_bank(v + 1, out=spread[name][:], in_=bank[:])
+
+        def spread_row_vectors():
+            names = list(row_vectors)
+            for first in range(0, len(names), 2):
+                bank = bank_pool.tile([P, 2 * H], BF16, name="bank")
+                pair = keep.tile([P, 2 * H], BF16, name="spread%d" % first)
+                for v in (0, 1):
+                    nc.tensor.matmul(
+                        out=bank[:, v * H : (v + 1) * H], lhsT=ones[:],
+                        rhs=vector_rows[:, (first + v) * H : (first + v + 1) * H],
+                        start=True, stop=True,
+                    )
+                    spread[names[first + v]] = pair[:, v * H : (v + 1) * H]
+                nc.vector.tensor_copy(out=pair[:], in_=bank[:])
 
         half_previous = {}
         for name in previous:
@@ -166,24 +184,32 @@ def tile_slstmcell_k_kernel(
         full = {}
         for name in (
             "tanh_f", "f_c", "f_n", "f_m", "i", "denominator", "reciprocal", "n_t", "z", "i_z",
-            "abs_i_z", "c_t", "m_t", "half_ratio", "tanh_o", "h", "centred", "h_t",
+            "larger", "c_t", "m_t", "half_ratio", "tanh_o", "h", "centred", "h_t",
         ):
             full[name] = keep.tile([P, H], F32, name=name)
         stats = keep.tile([P, BLOCKS_PER_GATE, 6], F32, name="stats")
+        function_of = {"f": ACT.Tanh, "i": ACT.Exp, "z": ACT.Tanh, "o": ACT.Tanh}
+        scale_of = {"f": 0.5, "i": 1.0, "z": 1.0, "o": 0.5}
+        result_of = {"f": "tanh_f", "i": "i", "z": "z", "o": "tanh_o"}
 
-        def activate(gate, cols, sums):
-            biased = small_pool.tile([P, P], F32, name="biased")
-            nc.vector.tensor_add(out=biased[:], in0=sums[:], in1=spread[gate][:, cols])
-            if gate == "f":
-                nc.scalar.activation(out=full["tanh_f"][:, cols], in_=biased[:], func=ACT.Tanh, scale=0.5)
-            if gate == "i":
-                nc.scalar.activation(out=full["i"][:, cols], in_=biased[:], func=ACT.Exp)
-            if gate == "z":
-                nc.scalar.activation(out=full["z"][:, cols], in_=biased[:], func=ACT.Tanh)
-            if gate == "o":
-                nc.scalar.activation(out=full["tanh_o"][:, cols], in_=biased[:], func=ACT.Tanh, scale=0.5)
+        def gate_and_columns(block):
+            gate, j = divmod(block, BLOCKS_PER_GATE)
+            return GATES[gate], j, slice(j * P, (j + 1) * P)
 
-        def combine(gate, j, cols):
+        def add_bias(block):
+            gate, j, cols = gate_and_columns(block)
+            biased[block] = small_pool.tile([P, P], F32, name="biased")
+            nc.vector.tensor_add(out=biased[block][:], in0=sums[block][:], in1=spread[gate][:, cols])
+
+        def apply_function(block):
+            gate, j, cols = gate_and_columns(block)
+            nc.scalar.activation(
+                out=full[result_of[gate]][:, cols], in_=biased[block][:],
+                func=function_of[gate], scale=scale_of[gate],
+            )
+
+        def combine(block):
+            gate, j, cols = gate_and_columns(block)
             if gate == "f":
                 for name in previous:
                     nc.vector.scalar_tensor_tensor(
@@ -203,77 +229,91 @@ def tile_slstmcell_k_kernel(
                 nc.vector.tensor_mul(
                     out=full["i_z"][:, cols], in0=full["i"][:, cols], in1=full["z"][:, cols]
                 )
-                nc.scalar.activation(out=full["abs_i_z"][:, cols], in_=full["i_z"][:, cols], func=ACT.Abs)
+                nc.vector.tensor_max(
+                    out=full["larger"][:, cols], in0=full["f_m"][:, cols], in1=full["i_z"][:, cols]
+                )
                 nc.vector.tensor_add(
                     out=full["c_t"][:, cols], in0=full["f_c"][:, cols], in1=full["i_z"][:, cols]
+                )
+                nc.vector.scalar_tensor_tensor(
+                    out=full["m_t"][:, cols], in0=full["i_z"][:, cols], scalar=-1.0,
+                    in1=full["larger"][:, cols], op0=ALU.mult, op1=ALU.max,
                 )
                 nc.vector.scalar_tensor_tensor(
                     out=full["half_ratio"][:, cols], in0=full["c_t"][:, cols], scalar=0.5,
                     in1=full["reciprocal"][:, cols], op0=ALU.mult, op1=ALU.mult,
                 )
-                nc.vector.tensor_max(
-                    out=full["m_t"][:, cols], in0=full["f_m"][:, cols], in1=full["abs_i_z"][:, cols]
-                )
+                if j == BLOCKS_PER_GATE - 1:
+                    nc.sync.dma_start(out=out_1, in_=full["c_t"][:])
+                    nc.sync.dma_start(out=out_2, in_=full["n_t"][:])
+                    nc.sync.dma_start(out=out_3, in_=full["m_t"][:])
             if gate == "o":
                 nc.vector.scalar_tensor_tensor(
                     out=full["h"][:, cols], in0=full["tanh_o"][:, cols], scalar=1.0,
                     in1=full["half_ratio"][:, cols], op0=ALU.add, op1=ALU.mult,
                 )
                 nc.vector.bn_stats(out=stats[:, j, :], in_=full["h"][:, cols])
-            if j == BLOCKS_PER_GATE - 1:
-                if gate == "i":
-                    nc.sync.dma_start(out=out_2, in_=full["n_t"][:])
-                if gate == "z":
-                    nc.sync.dma_start(out=out_1, in_=full["c_t"][:])
-                    nc.sync.dma_start(out=out_3, in_=full["m_t"][:])
 
-        def block_of(t):
-            gate, j = divmod(t // SLABS_PER_BLOCK, BLOCKS_PER_GATE)
-            return GATES[gate], j, slice(j * P, (j + 1) * P)
 
-        grouped_weights = {}
-        w_codes = {}
-        w_scales = {}
+        units = [[t] for t in range(len(pieces)) if pieces[t][0] < BLOCKS - 1]
+        units.append([t for t in range(len(pieces)) if pieces[t][0] == BLOCKS - 1])
+
+        def unit(number):
+            return units[number] if 0 <= number < len(units) else []
+
+        def finished_block(number):
+            for t in unit(number):
+                if pieces[t][1] + pieces[t][2] == PASSES:
+                    return pieces[t][0]
+            return None
+
+        grouped_of = {}
+        codes_of = {}
+        scales_of = {}
         sums = {}
-        for step in range(W_SLABS + 3):
-            if step + PREFETCH < W_SLABS:
-                raw_weights[step + PREFETCH] = load_weight_slab(step + PREFETCH)
-            if step < W_SLABS:
-                grouped_weights[step] = transpose_slab(raw_weights[step], step * BANKS_PER_SLAB)
+        biased = {}
+        for step in range(len(units) + MULTIPLY_LAG + 2):
+            left_for_vector = None
+            for t in unit(step):
+                block, first_pass, n_passes = pieces[t]
+                if t + PREFETCH < len(pieces):
+                    load_weight_piece(t + PREFETCH)
+                grouped_of[t], left = transpose_piece(block, first_pass, n_passes)
+                if left is not None:
+                    left_for_vector = left
 
-            t = step - 1
-            if 0 <= t < W_SLABS:
-                w_codes[t] = quantised_pool.tile([P, slab_words], U32, name="w_codes", align_bytes=64)
-                w_scales[t] = quantised_pool.tile([P, slab_words], U8, name="w_scales", align_bytes=64)
-                quantise_slab(grouped_weights[t], w_codes[t][:], w_scales[t][:])
+            for t in unit(step - 1):
+                n_words = pieces[t][2] * P
+                codes_of[t] = quantised_pool.tile([P, n_words], U32, name="w_codes", align_bytes=64)
+                scales_of[t] = quantised_pool.tile([P, n_words], U8, name="w_scales", align_bytes=64)
+                quantise_piece(grouped_of[t], codes_of[t][:], scales_of[t][:])
 
-            t = step - 2
-            if 0 <= t < W_SLABS:
-                block, s = divmod(t, SLABS_PER_BLOCK)
-                if s == 0:
+            if step == MULTIPLY_LAG:
+                spread_row_vectors()
+
+            for t in unit(step - MULTIPLY_LAG):
+                block, first_pass, n_passes = pieces[t]
+                if first_pass == 0:
                     sums[block] = sum_pool.tile([P, P], F32, name="sums")
-                for q in range(PASSES_PER_SLAB):
-                    k_pass = s * PASSES_PER_SLAB + q
-                    x_words = slice(k_pass * P, (k_pass + 1) * P)
+                for q in range(n_passes):
+                    x_words = slice((first_pass + q) * P, (first_pass + q + 1) * P)
                     w_words = slice(q * P, (q + 1) * P)
                     nc.tensor.matmul_mx(
                         out=sums[block][:],
                         lhsT=x_codes[:, x_words].bitcast(FP8X4),
                         lhsT_scale=x_scales[:, x_words],
-                        rhs=w_codes[t][:, w_words].bitcast(FP8X4),
-                        rhs_scale=w_scales[t][:, w_words],
-                        start=(k_pass == 0),
-                        stop=(k_pass == PASSES - 1),
+                        rhs=codes_of[t][:, w_words].bitcast(FP8X4),
+                        rhs_scale=scales_of[t][:, w_words],
+                        start=(first_pass + q == 0),
+                        stop=(first_pass + q == PASSES - 1),
                     )
 
-            t = step - 3
-            if 0 <= t < W_SLABS and t % SLABS_PER_BLOCK == SLABS_PER_BLOCK - 1:
-                gate, j, cols = block_of(t)
-                combine(gate, j, cols)
-            t = step - 2
-            if 0 <= t < W_SLABS and t % SLABS_PER_BLOCK == SLABS_PER_BLOCK - 1:
-                gate, j, cols = block_of(t)
-                activate(gate, cols, sums[t // SLABS_PER_BLOCK])
+            if finished_block(step - MULTIPLY_LAG - 1) is not None:
+                add_bias(finished_block(step - MULTIPLY_LAG - 1))
+                apply_function(finished_block(step - MULTIPLY_LAG - 1))
+            if finished_block(step - MULTIPLY_LAG - 2) is not None:
+                combine(finished_block(step - MULTIPLY_LAG - 2))
+            vector_empties(left_for_vector)
 
         mean_var = keep.tile([P, 2], F32, name="mean_var")
         nc.vector.bn_aggr(out=mean_var[:], in_=stats[:].rearrange("p j s -> p (j s)"))
@@ -283,10 +323,10 @@ def tile_slstmcell_k_kernel(
         nc.gpsimd.tensor_tensor(out=inv_std[:], in0=var_eps[:], in1=minus_half[:], op=ALU.pow)
         nc.vector.scalar_tensor_tensor(
             out=full["centred"][:], in0=full["h"][:], scalar=mean_var[:, 0:1],
-            in1=spread["gamma"][:], op0=ALU.subtract, op1=ALU.mult,
+            in1=spread["gamma"], op0=ALU.subtract, op1=ALU.mult,
         )
         nc.vector.scalar_tensor_tensor(
             out=full["h_t"][:], in0=full["centred"][:], scalar=inv_std[:],
-            in1=spread["beta"][:], op0=ALU.mult, op1=ALU.add,
+            in1=spread["beta"], op0=ALU.mult, op1=ALU.add,
         )
         nc.sync.dma_start(out=out_0, in_=full["h_t"][:])

@@ -31,7 +31,6 @@ BLOCKS = len(GATES) * BLOCKS_PER_GATE
 
 TRANSPOSE_BANKS = 6
 PREFETCH = 8
-MULTIPLY_LAG = 2
 
 FLOPS = 2 * P * D * len(GATES) * H
 
@@ -255,65 +254,66 @@ def tile_slstmcell_k_kernel(
                 nc.vector.bn_stats(out=stats[:, j, :], in_=full["h"][:, cols])
 
 
-        units = [[t] for t in range(len(pieces)) if pieces[t][0] < BLOCKS - 1]
-        units.append([t for t in range(len(pieces)) if pieces[t][0] == BLOCKS - 1])
-
-        def unit(number):
-            return units[number] if 0 <= number < len(units) else []
-
-        def finished_block(number):
-            for t in unit(number):
-                if pieces[t][1] + pieces[t][2] == PASSES:
-                    return pieces[t][0]
-            return None
-
         grouped_of = {}
         codes_of = {}
         scales_of = {}
         sums = {}
         biased = {}
-        for step in range(len(units) + MULTIPLY_LAG + 2):
-            left_for_vector = None
-            for t in unit(step):
-                block, first_pass, n_passes = pieces[t]
-                if t + PREFETCH < len(pieces):
-                    load_weight_piece(t + PREFETCH)
-                grouped_of[t], left = transpose_piece(block, first_pass, n_passes)
-                if left is not None:
-                    left_for_vector = left
 
-            for t in unit(step - 1):
-                n_words = pieces[t][2] * P
-                codes_of[t] = quantised_pool.tile([P, n_words], U32, name="w_codes", align_bytes=64)
-                scales_of[t] = quantised_pool.tile([P, n_words], U8, name="w_scales", align_bytes=64)
-                quantise_piece(grouped_of[t], codes_of[t][:], scales_of[t][:])
+        def quantise_weight_piece(t):
+            n_words = pieces[t][2] * P
+            codes_of[t] = quantised_pool.tile([P, n_words], U32, name="w_codes", align_bytes=64)
+            scales_of[t] = quantised_pool.tile([P, n_words], U8, name="w_scales", align_bytes=64)
+            quantise_piece(grouped_of[t], codes_of[t][:], scales_of[t][:])
 
-            if step == MULTIPLY_LAG:
-                spread_row_vectors()
-
-            for t in unit(step - MULTIPLY_LAG):
-                block, first_pass, n_passes = pieces[t]
-                if first_pass == 0:
-                    sums[block] = sum_pool.tile([P, P], F32, name="sums")
-                for q in range(n_passes):
-                    x_words = slice((first_pass + q) * P, (first_pass + q + 1) * P)
-                    w_words = slice(q * P, (q + 1) * P)
-                    nc.tensor.matmul_mx(
-                        out=sums[block][:],
-                        lhsT=x_codes[:, x_words].bitcast(FP8X4),
-                        lhsT_scale=x_scales[:, x_words],
-                        rhs=codes_of[t][:, w_words].bitcast(FP8X4),
-                        rhs_scale=scales_of[t][:, w_words],
-                        start=(first_pass + q == 0),
-                        stop=(first_pass + q == PASSES - 1),
-                    )
-
-            if finished_block(step - MULTIPLY_LAG - 1) is not None:
-                add_bias(finished_block(step - MULTIPLY_LAG - 1))
-                apply_function(finished_block(step - MULTIPLY_LAG - 1))
-            if finished_block(step - MULTIPLY_LAG - 2) is not None:
-                combine(finished_block(step - MULTIPLY_LAG - 2))
+        def bring_in(t):
+            block, first_pass, n_passes = pieces[t]
+            if t + PREFETCH < len(pieces):
+                load_weight_piece(t + PREFETCH)
+            grouped_of[t], left_for_vector = transpose_piece(block, first_pass, n_passes)
+            if t > 0:
+                quantise_weight_piece(t - 1)
             vector_empties(left_for_vector)
+
+        def multiply(block):
+            sums[block] = sum_pool.tile([P, P], F32, name="sums")
+            for t in range(len(pieces)):
+                if pieces[t][0] == block:
+                    first_pass, n_passes = pieces[t][1], pieces[t][2]
+                    for q in range(n_passes):
+                        x_words = slice((first_pass + q) * P, (first_pass + q + 1) * P)
+                        w_words = slice(q * P, (q + 1) * P)
+                        nc.tensor.matmul_mx(
+                            out=sums[block][:],
+                            lhsT=x_codes[:, x_words].bitcast(FP8X4),
+                            lhsT_scale=x_scales[:, x_words],
+                            rhs=codes_of[t][:, w_words].bitcast(FP8X4),
+                            rhs_scale=scales_of[t][:, w_words],
+                            start=(first_pass + q == 0),
+                            stop=(first_pass + q == PASSES - 1),
+                        )
+
+        for step in range(BLOCKS + 2):
+            own_pieces = [t for t in range(len(pieces)) if pieces[t][0] == step]
+            if step == BLOCKS:
+                quantise_weight_piece(len(pieces) - 1)
+            if step >= 2:
+                add_bias(step - 2)
+            for t in own_pieces[:1]:
+                bring_in(t)
+            if step >= 2:
+                apply_function(step - 2)
+            for t in own_pieces[1:]:
+                bring_in(t)
+            if step >= 2:
+                combine(step - 2)
+            if step == 1:
+                spread_row_vectors()
+            if 1 <= step <= BLOCKS:
+                multiply(step - 1)
+        add_bias(BLOCKS - 1)
+        apply_function(BLOCKS - 1)
+        combine(BLOCKS - 1)
 
         mean_var = keep.tile([P, 2], F32, name="mean_var")
         nc.vector.bn_aggr(out=mean_var[:], in_=stats[:].rearrange("p j s -> p (j s)"))

from contextlib import ExitStack

import concourse.mybir as mybir
from concourse.masks import make_identity

F32 = mybir.dt.float32
BF16 = mybir.dt.bfloat16
I32 = mybir.dt.int32
U32 = mybir.dt.uint32
U8 = mybir.dt.uint8
FP8X4 = mybir.dt.float8_e4m3fn_x4
ALU = mybir.AluOpType
ACT = mybir.ActivationFunctionType

P = 128
IN = 7680
H = 512
D = IN + H
LN_EPS = 1e-5
DIV_EPS = 1e-6

PACK = 4
K_PASS = P * PACK
PASSES = D // K_PASS
BANK_WORDS = 512
PASSES_PER_BANK = BANK_WORDS // (2 * P)

GATES = ("f", "i", "z", "o")
BLOCKS_PER_GATE = H // P
BLOCKS = len(GATES) * BLOCKS_PER_GATE

TRANSPOSE_BANKS = 6
PREFETCH = 8

FLOPS = 2 * P * D * len(GATES) * H


def piece_sizes(taper):
    sizes = [PASSES // 2]
    rest = PASSES // 2
    while taper and rest > PASSES_PER_BANK:
        rest = rest // 2
        sizes.append(rest)
    sizes.append(rest)
    return sizes


def tile_slstmcell_k_kernel(
    tc, x, h_prev, c_prev, n_prev, m_prev, Wi, bi, Wf, bf, Wo, bo, Wz, bz, ln_gamma, ln_beta,
    out_0, out_1, out_2, out_3,
):
    nc = tc.nc
    weights = {"f": Wf, "i": Wi, "z": Wz, "o": Wo}
    row_vectors = {"f": bf, "i": bi, "z": bz, "o": bo, "gamma": ln_gamma, "beta": ln_beta}
    previous = {"c": c_prev, "n": n_prev, "m": m_prev}

    with ExitStack() as ctx:
        ctx.enter_context(tc.manual_schedule())
        keep = ctx.enter_context(tc.tile_pool(name="keep", bufs=1))
        raw_pool = ctx.enter_context(tc.tile_pool(name="raw", bufs=PREFETCH + 2))
        grouped_pool = ctx.enter_context(tc.tile_pool(name="grouped", bufs=5))
        quantised_pool = ctx.enter_context(tc.tile_pool(name="quantised", bufs=5))
        small_pool = ctx.enter_context(tc.tile_pool(name="small", bufs=3))
        bank_pool = ctx.enter_context(tc.psum_pool(name="banks", bufs=TRANSPOSE_BANKS))
        sum_pool = ctx.enter_context(tc.psum_pool(name="sums", bufs=2))

        identity = keep.tile([P, P], F32, name="identity")
        make_identity(nc, identity[:])
        ones = keep.tile([P, P], BF16, name="ones")
        nc.vector.memset(ones[:], 1.0)
        minus_half = keep.tile([P, 1], F32, name="minus_half")
        nc.vector.memset(minus_half[:], -0.5)
        vector_rows = keep.tile([P, len(row_vectors) * H], BF16, name="vector_rows")
        nc.vector.memset(vector_rows[:].bitcast(I32), 0)
        table_warmer = keep.tile([P, 1], F32, name="table_warmer")
        nc.scalar.activation(out=table_warmer[:], in_=minus_half[:], func=ACT.Tanh)

        for v, name in enumerate(row_vectors):
            nc.gpsimd.dma_start(
                out=vector_rows[0:1, v * H : (v + 1) * H], in_=row_vectors[name].unsqueeze(0)
            )
        previous_bf16 = {}
        for name in previous:
            previous_bf16[name] = keep.tile([P, H], BF16, name="previous_" + name)
            nc.gpsimd.dma_start(out=previous_bf16[name][:], in_=previous[name])

        pieces = []
        for block in range(BLOCKS):
            first_pass = 0
            for n_passes in piece_sizes(block == BLOCKS - 1):
                pieces.append((block, first_pass, n_passes))
                first_pass += n_passes

        raw_at = {}

        def load_rows(block, first_pass, n_passes, sources):
            raw = raw_pool.tile([P, n_passes * K_PASS], BF16, name="raw")
            column = 0
            for source in sources:
                nc.sync.dma_start(out=raw[:, column : column + source.shape[1]], in_=source)
                column += source.shape[1]
            for q in range(n_passes):
                raw_at[(block, first_pass + q)] = (raw, q * K_PASS)

        def load_weight_piece(t):
            block, first_pass, n_passes = pieces[t]
            gate, j = divmod(block, BLOCKS_PER_GATE)
            k_range = slice(first_pass * K_PASS, (first_pass + n_passes) * K_PASS)
            load_rows(block, first_pass, n_passes, [weights[GATES[gate]][j * P : (j + 1) * P, k_range]])

        COMBINED = -1
        half_k = D // 2
        load_rows(COMBINED, 0, PASSES // 2, [x[:, 0:half_k]])
        load_rows(COMBINED, PASSES // 2, PASSES // 2, [x[:, half_k:IN], h_prev])
        for t in range(PREFETCH):
            load_weight_piece(t)

        def transpose_piece(block, first_pass, n_passes):
            grouped = grouped_pool.tile([P, n_passes * K_PASS], BF16, name="grouped", align_bytes=64)
            grouped_words = grouped[:].bitcast(F32)
            n_banks = n_passes // PASSES_PER_BANK
            left_for_vector = None
            for b in range(n_banks):
                bank = bank_pool.tile([P, 2, BANK_WORDS // 2], F32, name="bank")
                for g in range(PASSES_PER_BANK):
                    raw, column = raw_at[(block, first_pass + b * PASSES_PER_BANK + g)]
                    pass_words = raw[:, column : column + K_PASS].bitcast(F32)
                    for u in range(2):
                        nc.tensor.transpose(
                            bank[:, u, g * P : (g + 1) * P],
                            pass_words[:, u * P : (u + 1) * P],
                            identity[:],
                        )
                out = grouped_words[:, b * BANK_WORDS : (b + 1) * BANK_WORDS].rearrange(
                    "p (c u) -> p c u", u=2
                )
                in_ = bank[:].rearrange("p u c -> p c u")
                if b == n_banks - 1 and first_pass == 0:
                    left_for_vector = (out, in_)
                else:
                    nc.scalar.copy(out=out, in_=in_)
            return grouped, left_for_vector

        def vector_empties(left_for_vector):
            if left_for_vector is not None:
                nc.vector.tensor_copy(out=left_for_vector[0], in_=left_for_vector[1])

        def quantise_piece(grouped, codes, scales):
            nc.vector.quantize_mx(out=codes.bitcast(FP8X4), scales=scales, in_=grouped[:])

        x_codes = keep.tile([P, PASSES * P], U32, name="x_codes", align_bytes=64)
        x_scales = keep.tile([P, PASSES * P], U8, name="x_scales", align_bytes=64)
        for first_pass in (0, PASSES // 2):
            grouped, left_for_vector = transpose_piece(COMBINED, first_pass, PASSES // 2)
            vector_empties(left_for_vector)
            words = slice(first_pass * P, (first_pass + PASSES // 2) * P)
            quantise_piece(grouped, x_codes[:, words], x_scales[:, words])

        spread = {}

        def spread_row_vectors():
            names = list(row_vectors)
            for first in range(0, len(names), 2):
                bank = bank_pool.tile([P, 2 * H], BF16, name="bank")
                pair = keep.tile([P, 2 * H], BF16, name="spread%d" % first)
                for v in (0, 1):
                    nc.tensor.matmul(
                        out=bank[:, v * H : (v + 1) * H], lhsT=ones[:],
                        rhs=vector_rows[:, (first + v) * H : (first + v + 1) * H],
                        start=True, stop=True,
                    )
                    spread[names[first + v]] = pair[:, v * H : (v + 1) * H]
                nc.vector.tensor_copy(out=pair[:], in_=bank[:])

        half_previous = {}
        for name in previous:
            half_previous[name] = keep.tile([P, H], F32, name="half_previous_" + name)
            nc.gpsimd.tensor_scalar(
                out=half_previous[name][:], in0=previous_bf16[name][:],
                scalar1=0.5, scalar2=0.0, op0=ALU.mult, op1=ALU.add,
            )

        full = {}
        for name in (
            "tanh_f", "f_c", "f_n", "f_m", "i", "denominator", "reciprocal", "n_t", "z", "i_z",
            "larger", "c_t", "m_t", "half_ratio", "tanh_o", "h", "centred", "h_t",
        ):
            full[name] = keep.tile([P, H], F32, name=name)
        stats = keep.tile([P, BLOCKS_PER_GATE, 6], F32, name="stats")
        function_of = {"f": ACT.Tanh, "i": ACT.Exp, "z": ACT.Tanh, "o": ACT.Tanh}
        scale_of = {"f": 0.5, "i": 1.0, "z": 1.0, "o": 0.5}
        result_of = {"f": "tanh_f", "i": "i", "z": "z", "o": "tanh_o"}

        def gate_and_columns(block):
            gate, j = divmod(block, BLOCKS_PER_GATE)
            return GATES[gate], j, slice(j * P, (j + 1) * P)

        def add_bias(block):
            gate, j, cols = gate_and_columns(block)
            biased[block] = small_pool.tile([P, P], F32, name="biased")
            nc.vector.tensor_add(out=biased[block][:], in0=sums[block][:], in1=spread[gate][:, cols])

        def apply_function(block):
            gate, j, cols = gate_and_columns(block)
            nc.scalar.activation(
                out=full[result_of[gate]][:, cols], in_=biased[block][:],
                func=function_of[gate], scale=scale_of[gate],
            )

        def combine(block):
            gate, j, cols = gate_and_columns(block)
            if gate == "f":
                for name in previous:
                    nc.vector.scalar_tensor_tensor(
                        out=full["f_" + name][:, cols], in0=full["tanh_f"][:, cols], scalar=1.0,
                        in1=half_previous[name][:, cols], op0=ALU.add, op1=ALU.mult,
                    )
            if gate == "i":
                nc.vector.scalar_tensor_tensor(
                    out=full["denominator"][:, cols], in0=full["i"][:, cols], scalar=DIV_EPS,
                    in1=full["f_n"][:, cols], op0=ALU.add, op1=ALU.add,
                )
                nc.vector.tensor_add(
                    out=full["n_t"][:, cols], in0=full["f_n"][:, cols], in1=full["i"][:, cols]
                )
                nc.vector.reciprocal(out=full["reciprocal"][:, cols], in_=full["denominator"][:, cols])
            if gate == "z":
                nc.vector.tensor_mul(
                    out=full["i_z"][:, cols], in0=full["i"][:, cols], in1=full["z"][:, cols]
                )
                nc.vector.tensor_max(
                    out=full["larger"][:, cols], in0=full["f_m"][:, cols], in1=full["i_z"][:, cols]
                )
                nc.vector.tensor_add(
                    out=full["c_t"][:, cols], in0=full["f_c"][:, cols], in1=full["i_z"][:, cols]
                )
                nc.vector.scalar_tensor_tensor(
                    out=full["m_t"][:, cols], in0=full["i_z"][:, cols], scalar=-1.0,
                    in1=full["larger"][:, cols], op0=ALU.mult, op1=ALU.max,
                )
                nc.vector.scalar_tensor_tensor(
                    out=full["half_ratio"][:, cols], in0=full["c_t"][:, cols], scalar=0.5,
                    in1=full["reciprocal"][:, cols], op0=ALU.mult, op1=ALU.mult,
                )
                if j == BLOCKS_PER_GATE - 1:
                    nc.sync.dma_start(out=out_1, in_=full["c_t"][:])
                    nc.sync.dma_start(out=out_2, in_=full["n_t"][:])
                    nc.sync.dma_start(out=out_3, in_=full["m_t"][:])
            if gate == "o":
                nc.vector.scalar_tensor_tensor(
                    out=full["h"][:, cols], in0=full["tanh_o"][:, cols], scalar=1.0,
                    in1=full["half_ratio"][:, cols], op0=ALU.add, op1=ALU.mult,
                )
                nc.vector.bn_stats(out=stats[:, j, :], in_=full["h"][:, cols])


        grouped_of = {}
        codes_of = {}
        scales_of = {}
        sums = {}
        biased = {}

        def quantise_weight_piece(t):
            n_words = pieces[t][2] * P
            codes_of[t] = quantised_pool.tile([P, n_words], U32, name="w_codes", align_bytes=64)
            scales_of[t] = quantised_pool.tile([P, n_words], U8, name="w_scales", align_bytes=64)
            quantise_piece(grouped_of[t], codes_of[t][:], scales_of[t][:])

        def bring_in(t):
            block, first_pass, n_passes = pieces[t]
            if t + PREFETCH < len(pieces):
                load_weight_piece(t + PREFETCH)
            grouped_of[t], left_for_vector = transpose_piece(block, first_pass, n_passes)
            if t > 0:
                quantise_weight_piece(t - 1)
            vector_empties(left_for_vector)

        def multiply(block):
            sums[block] = sum_pool.tile([P, P], F32, name="sums")
            for t in range(len(pieces)):
                if pieces[t][0] == block:
                    first_pass, n_passes = pieces[t][1], pieces[t][2]
                    for q in range(n_passes):
                        x_words = slice((first_pass + q) * P, (first_pass + q + 1) * P)
                        w_words = slice(q * P, (q + 1) * P)
                        nc.tensor.matmul_mx(
                            out=sums[block][:],
                            lhsT=x_codes[:, x_words].bitcast(FP8X4),
                            lhsT_scale=x_scales[:, x_words],
                            rhs=codes_of[t][:, w_words].bitcast(FP8X4),
                            rhs_scale=scales_of[t][:, w_words],
                            start=(first_pass + q == 0),
                            stop=(first_pass + q == PASSES - 1),
                        )

        for step in range(BLOCKS + 2):
            own_pieces = [t for t in range(len(pieces)) if pieces[t][0] == step]
            if step == BLOCKS:
                quantise_weight_piece(len(pieces) - 1)
            if step >= 2:
                add_bias(step - 2)
            for t in own_pieces[:1]:
                bring_in(t)
            if step >= 2:
                apply_function(step - 2)
            for t in own_pieces[1:]:
                bring_in(t)
            if step >= 2:
                combine(step - 2)
            if step == 1:
                spread_row_vectors()
            if 1 <= step <= BLOCKS:
                multiply(step - 1)
        add_bias(BLOCKS - 1)
        apply_function(BLOCKS - 1)
        combine(BLOCKS - 1)

        mean_var = keep.tile([P, 2], F32, name="mean_var")
        nc.vector.bn_aggr(out=mean_var[:], in_=stats[:].rearrange("p j s -> p (j s)"))
        var_eps = keep.tile([P, 1], F32, name="var_eps")
        nc.vector.tensor_scalar_add(out=var_eps[:], in0=mean_var[:, 1:2], scalar1=LN_EPS)
        inv_std = keep.tile([P, 1], F32, name="inv_std")
        nc.gpsimd.tensor_tensor(out=inv_std[:], in0=var_eps[:], in1=minus_half[:], op=ALU.pow)
        nc.vector.scalar_tensor_tensor(
            out=full["centred"][:], in0=full["h"][:], scalar=mean_var[:, 0:1],
            in1=spread["gamma"], op0=ALU.subtract, op1=ALU.mult,
        )
        nc.vector.scalar_tensor_tensor(
            out=full["h_t"][:], in0=full["centred"][:], scalar=inv_std[:],
            in1=spread["beta"], op0=ALU.mult, op1=ALU.add,
        )
        nc.sync.dma_start(out=out_0, in_=full["h_t"][:])
